import numpy as np
import ml_dtypes


def mxq(x, axis, fmt="e4m3"):
    dtype, down = {"e4m3": (ml_dtypes.float8_e4m3fn, 7), "e5m2": (ml_dtypes.float8_e5m2, 14)}[fmt]
    v = np.moveaxis(np.asarray(x, np.float32).astype(ml_dtypes.bfloat16).astype(np.float64), axis, -1)
    blocks = v.reshape(v.shape[:-1] + (-1, 32))
    amax = np.abs(blocks).max(-1, keepdims=True)
    byte = np.maximum(np.where(amax > 0, np.frexp(amax)[1] - 1 + 127, 0) - down, 1)
    scale = np.exp2(byte - 127.0)
    codes = (blocks / scale).astype(np.float32).astype(dtype).astype(np.float64)
    return np.moveaxis((codes * scale).reshape(v.shape), -1, axis)


WIDE = False


def mx_kscale(k):
    if not WIDE:
        return np.ones(k)
    levels = np.array([10, -10, 5, -5, 0])
    a = np.random.permutation(np.resize(levels, k // 512 * 4)).reshape(k // 512, 4)
    idx = np.arange(k)
    return np.exp2(a[idx // 512, idx % 128 // 32])


BF16 = ml_dtypes.bfloat16


def bf(x):
    return np.asarray(x, np.float32).astype(BF16)


def f64(x):
    return np.asarray(x).astype(np.float64)


B, IN, OUT = 512, 2048, 2048


def setup_inputs():
    s = mx_kscale(IN)
    return {"input_data": bf(np.random.standard_normal((B, IN)) * s),
            "weight": bf(np.random.standard_normal((OUT, IN)) / np.sqrt(IN) / s),
            "bias": bf(np.random.standard_normal(OUT) * 0.5),
            "prev_grad": bf(np.random.standard_normal((OUT, IN)) / np.sqrt(IN) / s),
            "prev_bias_grad": bf(np.random.standard_normal(OUT) * 0.5),
            "lr_samples": bf(np.random.uniform(0.1, 1.0, B))}


def reference(input_data, weight, bias, prev_grad, prev_bias_grad, lr_samples):
    xq = mxq(f64(input_data), 1, "e4m3")
    base = (xq @ mxq(f64(weight), 1, "e4m3").T) + f64(bias)
    pert = (xq @ mxq(f64(prev_grad), 1, "e4m3").T) + f64(prev_bias_grad)
    return base - f64(lr_samples)[:, None] * pert

@@ -1,0 +1,241 @@
+from contextlib import ExitStack
+
+import concourse.masks as masks
+import concourse.mybir as mybir
+
+F32 = mybir.dt.float32
+BF16 = mybir.dt.bfloat16
+U32 = mybir.dt.uint32
+U8 = mybir.dt.uint8
+FP8X4 = mybir.dt.float8_e4m3fn_x4
+ALU = mybir.AluOpType
+
+P = 128
+B = 512
+K = 2048
+O = 2048
+PASSES = K // 512
+NBT = B // P
+CHUNK = 512
+FLOPS = 2 * 2 * B * K * O
+
+RAW_BUFS = 5
+
+
+def tile_optimizedlinear_kernel(
+    tc, input_data, weight, bias, prev_grad, prev_bias_grad, lr_samples, out
+):
+    nc = tc.nc
+    with ExitStack() as ctx:
+        consts = ctx.enter_context(tc.tile_pool(name="consts", bufs=1))
+        rawp = ctx.enter_context(tc.tile_pool(name="rawp", bufs=RAW_BUFS))
+        grpp = ctx.enter_context(tc.tile_pool(name="grpp", bufs=2))
+        codp = ctx.enter_context(tc.tile_pool(name="codp", bufs=3))
+        cpool = ctx.enter_context(tc.tile_pool(name="cpool", bufs=2))
+        opool = ctx.enter_context(tc.tile_pool(name="opool", bufs=2))
+        psum = ctx.enter_context(tc.psum_pool(name="psum", bufs=8))
+        ctx.enter_context(tc.manual_schedule())
+
+        x_v = input_data.rearrange("(t p) k -> p t k", p=P)
+        w_v = weight.rearrange("(t p) k -> p t k", p=P)
+        g_v = prev_grad.rearrange("(t p) k -> p t k", p=P)
+
+        units = [("x", x_v, 0, 2), ("x", x_v, 2, 2)]
+        units += [("w", w_v, 0, 2), ("w", w_v, 2, 2), ("g", g_v, 0, 2), ("g", g_v, 2, 2)]
+        for ch in range(1, O // CHUNK):
+            units += [("w", w_v, 4 * ch, 4), ("g", g_v, 4 * ch, 4)]
+        n_units = len(units)
+
+        ident = consts.tile([P, P], F32)
+        masks.make_identity(nc, ident[:])
+        ident_bf = consts.tile([P, P], BF16)
+        masks.make_identity(nc, ident_bf[:])
+        rows = consts.tile([P, CHUNK], BF16)
+        nc.vector.memset(rows[:], 0.0)
+        nc.sync.dma_start(out=rows[0:4, :], in_=bias.rearrange("(r n) -> r n", n=CHUNK))
+        nc.sync.dma_start(out=rows[4:8, :], in_=prev_bias_grad.rearrange("(r n) -> r n", n=CHUNK))
+        nc.sync.dma_start(out=rows[8:12, 0:P], in_=lr_samples.rearrange("(t p) -> t p", p=P))
+        neg_lr = consts.tile([P, NBT], F32)
+        bias_bc = consts.tile([P, O], F32)
+        pbias_bc = consts.tile([P, O], F32)
+
+        raws = {}
+
+        def load(i):
+            kind, view, t0, n = units[i]
+            raw = rawp.tile([P, 4, K], BF16, name="raw%d" % i, tag="raw")
+            nc.sync.dma_start(out=raw[:, 0:n, :], in_=view[:, t0 : t0 + n, :])
+            raws[i] = raw
+
+        grouped = {}
+        codes = {}
+        planes = {}
+
+        def transposes(i, pattern):
+            kind, view, t0, n = units[i]
+            width = n * P
+            raw_w = raws[i][:].bitcast(F32)
+            grp = grpp.tile([P, PASSES, 4 * width], BF16, name="grp%d" % i, tag="grp", align_bytes=64)
+            grouped[i] = grp
+            grp_w = grp[:].bitcast(F32)
+            b = 0
+            for g in range(PASSES):
+                for h in range(n // 2):
+                    bank = psum.tile([P, 512], F32, name="bank%d_%d" % (i, b), tag="ps")
+                    for j in range(2):
+                        for u in range(2):
+                            s = 2 * j + u
+                            c0 = 256 * g + 128 * u
+                            nc.tensor.transpose(
+                                bank[:, s * P : (s + 1) * P], raw_w[:, 2 * h + j, c0 : c0 + P], ident[:]
+                            )
+                    dst = grp_w[:, g, 512 * h : 512 * h + 512].rearrange("p (j o u) -> p j o u", j=2, u=2)
+                    src = bank[:].rearrange("p (j u o) -> p j o u", j=2, u=2)
+                    if pattern[b % len(pattern)] == "S":
+                        nc.scalar.copy(out=dst, in_=src)
+                    else:
+                        nc.vector.tensor_copy(out=dst, in_=src)
+                    b += 1
+
+        def alloc_codes(i):
+            kind, view, t0, n = units[i]
+            width = n * P
+            if kind == "x":
+                cod = consts.tile([P, PASSES, width], U32, name="xcod%d" % i, align_bytes=64)
+                pla = consts.tile([P, PASSES, width], U8, name="xpla%d" % i, align_bytes=64)
+            else:
+                cod = codp.tile([P, PASSES, width], U32, name="cod%d" % i, tag="cod", align_bytes=64)
+                pla = codp.tile([P, PASSES, width], U8, name="pla%d" % i, tag="pla", align_bytes=64)
+            codes[i] = cod
+            planes[i] = pla
+
+        def quantise(i, g0):
+            if g0 == 0:
+                alloc_codes(i)
+            nc.vector.quantize_mx(
+                out=codes[i][:, g0 : g0 + 2, :].rearrange("p g n -> p (g n)").bitcast(FP8X4),
+                scales=planes[i][:, g0 : g0 + 2, :].rearrange("p g n -> p (g n)"),
+                in_=grouped[i][:, g0 : g0 + 2, :].rearrange("p g c -> p (g c)"),
+            )
+
+        c_tiles = {}
+        o_tiles = {}
+
+        def c_job(ch, bt):
+            if ch not in c_tiles:
+                c_tiles[ch] = cpool.tile([P, NBT, CHUNK], F32, name="c%d" % ch, tag="c")
+            cols = slice(ch * CHUNK, (ch + 1) * CHUNK)
+            nc.vector.scalar_tensor_tensor(
+                out=c_tiles[ch][:, bt, :],
+                in0=pbias_bc[:, cols],
+                scalar=neg_lr[:, bt : bt + 1],
+                in1=bias_bc[:, cols],
+                op0=ALU.mult,
+                op1=ALU.add,
+            )
+
+        def mx_group(i, bt, first=0, width=None):
+            kind, view, t0, n = units[i]
+            if width is None:
+                width = n * P
+            acc = psum.tile([P, 512], F32, name="acc%d_%d_%d" % (i, bt, first), tag="ps")
+            xi = bt // 2
+            xs = slice((bt % 2) * P, (bt % 2) * P + P)
+            for g in range(PASSES):
+                nc.tensor.matmul_mx(
+                    out=acc[:, 0:width],
+                    lhsT=codes[xi][:, g, xs].bitcast(FP8X4),
+                    lhsT_scale=planes[xi][:, g, xs],
+                    rhs=codes[i][:, g, first : first + width].bitcast(FP8X4),
+                    rhs_scale=planes[i][:, g, first : first + width],
+                    start=(g == 0),
+                    stop=(g == PASSES - 1),
+                )
+            ch = (t0 * P) // CHUNK
+            lo = t0 * P - ch * CHUNK + first
+            if ch not in o_tiles:
+                o_tiles[ch] = opool.tile([P, NBT, CHUNK], F32, name="o%d" % ch, tag="o")
+            o_sl = o_tiles[ch][:, bt, lo : lo + width]
+            if kind == "w":
+                nc.vector.tensor_tensor(
+                    out=o_sl, in0=acc[:, 0:width], in1=c_tiles[ch][:, bt, lo : lo + width], op=ALU.add
+                )
+            else:
+                nc.vector.scalar_tensor_tensor(
+                    out=o_sl,
+                    in0=acc[:, 0:width],
+                    scalar=neg_lr[:, bt : bt + 1],
+                    in1=o_sl,
+                    op0=ALU.mult,
+                    op1=ALU.add,
+                )
+                nc.sync.dma_start(
+                    out=out[bt * P : (bt + 1) * P, ch * CHUNK + lo : ch * CHUNK + lo + width], in_=o_sl
+                )
+
+        for i in range(RAW_BUFS):
+            load(i)
+
+        def next_load(i):
+            if i + RAW_BUFS < n_units:
+                load(i + RAW_BUFS)
+
+        lr_ps = psum.tile([P, 512], F32, name="lr_ps", tag="ps")
+        nc.tensor.matmul(out=lr_ps[:, 0:32], lhsT=rows[:, 0:P], rhs=ident_bf[:, 0:32], start=True, stop=True)
+        nc.vector.tensor_scalar_mul(out=neg_lr[:], in0=lr_ps[:, 8:12], scalar1=-1.0)
+
+        def spread(ch):
+            for r, dst_t, eng in ((ch, bias_bc, "S"), (4 + ch, pbias_bc, "V" if ch == 0 else "S")):
+                bc = psum.tile([P, 512], F32, name="bc%d" % r, tag="ps")
+                nc.tensor.matmul(
+                    out=bc[:], lhsT=ident_bf[:, r : r + 1].to_broadcast([P, P]), rhs=rows[:], start=True, stop=True
+                )
+                dst = dst_t[:, ch * CHUNK : (ch + 1) * CHUNK]
+                if eng == "S":
+                    nc.scalar.copy(out=dst, in_=bc[:])
+                else:
+                    nc.vector.tensor_copy(out=dst, in_=bc[:])
+
+        spread(0)
+        for bt in range(NBT):
+            c_job(0, bt)
+        for i in range(3):
+            transposes(i, "SV")
+            next_load(i)
+            quantise(i, 0)
+            quantise(i, 2)
+            spread(i + 1)
+
+        extra = {}
+        for i in range(2, n_units):
+            kind, view, t0, n = units[i]
+            ch = (t0 * P) // CHUNK
+            if ch + 1 >= O // CHUNK:
+                extra[i] = []
+            elif n == 2:
+                extra[i] = [(ch + 1, (0 if kind == "w" else 2) + (t0 % 4) // 2)]
+            else:
+                extra[i] = [(ch + 1, 0), (ch + 1, 1)] if kind == "w" else [(ch + 1, 2), (ch + 1, 3)]
+
+        for i in range(2, n_units):
+            nxt = i + 1
+            if nxt < n_units:
+                transposes(nxt, "S")
+                next_load(nxt)
+                quantise(nxt, 0)
+            jobs = extra[i]
+            if nxt == n_units:
+                for bt in range(NBT):
+                    mx_group(i, bt, 0, 256)
+                    mx_group(i, bt, 256, 256)
+                break
+            mx_group(i, 0)
+            if len(jobs) > 0:
+                c_job(jobs[0][0], jobs[0][1])
+            mx_group(i, 1)
+            if nxt < n_units:
+                quantise(nxt, 2)
+            mx_group(i, 2)
+            if len(jobs) > 1:
+                c_job(jobs[1][0], jobs[1][1])
+            mx_group(i, 3)

@@ -46,12 +46,12 @@ def tile_optimizedlinear_kernel(
             units += [("w", w_v, 4 * ch, 4), ("g", g_v, 4 * ch, 4)]
         n_units = len(units)
 
-        ident = consts.tile([P, P], F32)
-        masks.make_identity(nc, ident[:])
+        rows = consts.tile([P, CHUNK], BF16)
+        nc.gpsimd.memset(rows[:].bitcast(F32), 0.0)
         ident_bf = consts.tile([P, P], BF16)
         masks.make_identity(nc, ident_bf[:])
-        rows = consts.tile([P, CHUNK], BF16)
-        nc.vector.memset(rows[:], 0.0)
+        ident = consts.tile([P, P], F32)
+        masks.make_identity(nc, ident[:])
         nc.sync.dma_start(out=rows[0:4, :], in_=bias.rearrange("(r n) -> r n", n=CHUNK))
         nc.sync.dma_start(out=rows[4:8, :], in_=prev_bias_grad.rearrange("(r n) -> r n", n=CHUNK))
         nc.sync.dma_start(out=rows[8:12, 0:P], in_=lr_samples.rearrange("(t p) -> t p", p=P))

@@ -101,17 +101,28 @@ def tile_optimizedlinear_kernel(
             kind, view, t0, n = units[i]
             width = n * P
             if kind == "x":
-                cod = consts.tile([P, PASSES, width], U32, name="xcod%d" % i, align_bytes=64)
-                pla = consts.tile([P, PASSES, width], U8, name="xpla%d" % i, align_bytes=64)
+                cod = consts.tile([P, 48 + PASSES * width], U32, name="xcod%d" % i, align_bytes=256)
+                pla = consts.tile([P, PASSES, 2, 256], U8, name="xpla%d" % i, align_bytes=256)
+                codes[i] = cod[:, 48:].rearrange("p (g n) -> p g n", g=PASSES)
+                planes[i] = pla
             else:
-                cod = codp.tile([P, PASSES, width], U32, name="cod%d" % i, tag="cod", align_bytes=64)
-                pla = codp.tile([P, PASSES, width], U8, name="pla%d" % i, tag="pla", align_bytes=64)
-            codes[i] = cod
-            planes[i] = pla
+                cod = codp.tile([P, PASSES, width], U32, name="cod%d" % i, tag="cod", align_bytes=256)
+                pla = codp.tile([P, PASSES, width], U8, name="pla%d" % i, tag="pla", align_bytes=256)
+                codes[i] = cod
+                planes[i] = pla
 
         def quantise(i, g0):
             if g0 == 0:
                 alloc_codes(i)
+            if units[i][0] == "x":
+                for g in (g0, g0 + 1):
+                    for j in range(2):
+                        nc.vector.quantize_mx(
+                            out=codes[i][:, g, j * P : (j + 1) * P].bitcast(FP8X4),
+                            scales=planes[i][:, g, j, 0:P],
+                            in_=grouped[i][:, g, j * 4 * P : (j + 1) * 4 * P],
+                        )
+                return
             nc.vector.quantize_mx(
                 out=codes[i][:, g0 : g0 + 2, :].rearrange("p g n -> p (g n)").bitcast(FP8X4),
                 scales=planes[i][:, g0 : g0 + 2, :].rearrange("p g n -> p (g n)"),
@@ -145,7 +156,7 @@ def tile_optimizedlinear_kernel(
                 nc.tensor.matmul_mx(
                     out=acc[:, 0:width],
                     lhsT=codes[xi][:, g, xs].bitcast(FP8X4),
-                    lhsT_scale=planes[xi][:, g, xs],
+                    lhsT_scale=planes[xi][:, g, bt % 2, 0:P],
                     rhs=codes[i][:, g, first : first + width].bitcast(FP8X4),
                     rhs_scale=planes[i][:, g, first : first + width],
                     start=(g == 0),

@@ -31,7 +31,6 @@ def tile_optimizedlinear_kernel(
         rawp = ctx.enter_context(tc.tile_pool(name="rawp", bufs=RAW_BUFS))
         grpp = ctx.enter_context(tc.tile_pool(name="grpp", bufs=2))
         codp = ctx.enter_context(tc.tile_pool(name="codp", bufs=3))
-        cpool = ctx.enter_context(tc.tile_pool(name="cpool", bufs=2))
         opool = ctx.enter_context(tc.tile_pool(name="opool", bufs=2))
         psum = ctx.enter_context(tc.psum_pool(name="psum", bufs=8))
         ctx.enter_context(tc.manual_schedule())
@@ -46,18 +45,18 @@ def tile_optimizedlinear_kernel(
             units += [("w", w_v, 4 * ch, 4), ("g", g_v, 4 * ch, 4)]
         n_units = len(units)
 
-        rows = consts.tile([P, CHUNK], BF16)
-        nc.gpsimd.memset(rows[:].bitcast(F32), 0.0)
-        ident_bf = consts.tile([P, P], BF16)
-        masks.make_identity(nc, ident_bf[:])
+        lhs_c = consts.tile([P, B], BF16)
+        nc.gpsimd.memset(lhs_c[:].bitcast(F32), 0.0)
+        nc.gpsimd.memset(lhs_c[32:33, :], -1.0)
+        rhs_c = consts.tile([P, O + 32], BF16)
+        nc.vector.memset(rhs_c[:].bitcast(F32), 0.0)
+        nc.vector.memset(rhs_c[0:1, O : O + 32], -1.0)
+        nc.sync.dma_start(out=lhs_c[0:1, :], in_=lr_samples.rearrange("(o n) -> o n", o=1))
+        nc.sync.dma_start(out=rhs_c[0:1, 0:O], in_=prev_bias_grad.rearrange("(o n) -> o n", o=1))
+        nc.sync.dma_start(out=rhs_c[32:33, 0:O], in_=bias.rearrange("(o n) -> o n", o=1))
         ident = consts.tile([P, P], F32)
         masks.make_identity(nc, ident[:])
-        nc.sync.dma_start(out=rows[0:4, :], in_=bias.rearrange("(r n) -> r n", n=CHUNK))
-        nc.sync.dma_start(out=rows[4:8, :], in_=prev_bias_grad.rearrange("(r n) -> r n", n=CHUNK))
-        nc.sync.dma_start(out=rows[8:12, 0:P], in_=lr_samples.rearrange("(t p) -> t p", p=P))
         neg_lr = consts.tile([P, NBT], F32)
-        bias_bc = consts.tile([P, O], F32)
-        pbias_bc = consts.tile([P, O], F32)
 
         raws = {}
 
@@ -101,49 +100,42 @@ def tile_optimizedlinear_kernel(
             kind, view, t0, n = units[i]
             width = n * P
             if kind == "x":
-                cod = consts.tile([P, 48 + PASSES * width], U32, name="xcod%d" % i, align_bytes=256)
-                pla = consts.tile([P, PASSES, 2, 256], U8, name="xpla%d" % i, align_bytes=256)
-                codes[i] = cod[:, 48:].rearrange("p (g n) -> p g n", g=PASSES)
-                planes[i] = pla
+                cod = consts.tile([P, PASSES, width], U32, name="xcod%d" % i, align_bytes=64)
+                pla = consts.tile([P, PASSES, width], U8, name="xpla%d" % i, align_bytes=64)
             else:
-                cod = codp.tile([P, PASSES, width], U32, name="cod%d" % i, tag="cod", align_bytes=256)
-                pla = codp.tile([P, PASSES, width], U8, name="pla%d" % i, tag="pla", align_bytes=256)
-                codes[i] = cod
-                planes[i] = pla
+                cod = codp.tile([P, PASSES, width], U32, name="cod%d" % i, tag="cod", align_bytes=64)
+                pla = codp.tile([P, PASSES, width], U8, name="pla%d" % i, tag="pla", align_bytes=64)
+            codes[i] = cod
+            planes[i] = pla
 
         def quantise(i, g0):
             if g0 == 0:
                 alloc_codes(i)
-            if units[i][0] == "x":
-                for g in (g0, g0 + 1):
-                    for j in range(2):
-                        nc.vector.quantize_mx(
-                            out=codes[i][:, g, j * P : (j + 1) * P].bitcast(FP8X4),
-                            scales=planes[i][:, g, j, 0:P],
-                            in_=grouped[i][:, g, j * 4 * P : (j + 1) * 4 * P],
-                        )
-                return
             nc.vector.quantize_mx(
                 out=codes[i][:, g0 : g0 + 2, :].rearrange("p g n -> p (g n)").bitcast(FP8X4),
                 scales=planes[i][:, g0 : g0 + 2, :].rearrange("p g n -> p (g n)"),
                 in_=grouped[i][:, g0 : g0 + 2, :].rearrange("p g c -> p (g c)"),
             )
 
-        c_tiles = {}
+        d_tiles = {}
         o_tiles = {}
 
-        def c_job(ch, bt):
-            if ch not in c_tiles:
-                c_tiles[ch] = cpool.tile([P, NBT, CHUNK], F32, name="c%d" % ch, tag="c")
-            cols = slice(ch * CHUNK, (ch + 1) * CHUNK)
-            nc.vector.scalar_tensor_tensor(
-                out=c_tiles[ch][:, bt, :],
-                in0=pbias_bc[:, cols],
-                scalar=neg_lr[:, bt : bt + 1],
-                in1=bias_bc[:, cols],
-                op0=ALU.mult,
-                op1=ALU.add,
+        def d_job(n, eng):
+            ch, bt = n // NBT, n % NBT
+            if ch not in d_tiles:
+                d_tiles[ch] = consts.tile([P, NBT, CHUNK], F32, name="d%d" % ch)
+            d_ps = psum.tile([P, 512], F32, name="d_ps%d" % n, tag="ps")
+            nc.tensor.matmul(
+                out=d_ps[:],
+                lhsT=lhs_c[:, bt * P : (bt + 1) * P],
+                rhs=rhs_c[:, ch * CHUNK : (ch + 1) * CHUNK],
+                start=True,
+                stop=True,
             )
+            if eng == "S":
+                nc.scalar.copy(out=d_tiles[ch][:, bt, :], in_=d_ps[:])
+            else:
+                nc.vector.tensor_copy(out=d_tiles[ch][:, bt, :], in_=d_ps[:])
 
         def mx_group(i, bt, first=0, width=None):
             kind, view, t0, n = units[i]
@@ -156,7 +148,7 @@ def tile_optimizedlinear_kernel(
                 nc.tensor.matmul_mx(
                     out=acc[:, 0:width],
                     lhsT=codes[xi][:, g, xs].bitcast(FP8X4),
-                    lhsT_scale=planes[xi][:, g, bt % 2, 0:P],
+                    lhsT_scale=planes[xi][:, g, xs],
                     rhs=codes[i][:, g, first : first + width].bitcast(FP8X4),
                     rhs_scale=planes[i][:, g, first : first + width],
                     start=(g == 0),
@@ -169,7 +161,7 @@ def tile_optimizedlinear_kernel(
             o_sl = o_tiles[ch][:, bt, lo : lo + width]
             if kind == "w":
                 nc.vector.tensor_tensor(
-                    out=o_sl, in0=acc[:, 0:width], in1=c_tiles[ch][:, bt, lo : lo + width], op=ALU.add
+                    out=o_sl, in0=acc[:, 0:width], in1=d_tiles[ch][:, bt, lo : lo + width], op=ALU.subtract
                 )
             else:
                 nc.vector.scalar_tensor_tensor(
@@ -192,41 +184,25 @@ def tile_optimizedlinear_kernel(
                 load(i + RAW_BUFS)
 
         lr_ps = psum.tile([P, 512], F32, name="lr_ps", tag="ps")
-        nc.tensor.matmul(out=lr_ps[:, 0:32], lhsT=rows[:, 0:P], rhs=ident_bf[:, 0:32], start=True, stop=True)
-        nc.vector.tensor_scalar_mul(out=neg_lr[:], in0=lr_ps[:, 8:12], scalar1=-1.0)
-
-        def spread(ch):
-            for r, dst_t, eng in ((ch, bias_bc, "S"), (4 + ch, pbias_bc, "V" if ch == 0 else "S")):
-                bc = psum.tile([P, 512], F32, name="bc%d" % r, tag="ps")
-                nc.tensor.matmul(
-                    out=bc[:], lhsT=ident_bf[:, r : r + 1].to_broadcast([P, P]), rhs=rows[:], start=True, stop=True
-                )
-                dst = dst_t[:, ch * CHUNK : (ch + 1) * CHUNK]
-                if eng == "S":
-                    nc.scalar.copy(out=dst, in_=bc[:])
-                else:
-                    nc.vector.tensor_copy(out=dst, in_=bc[:])
-
-        spread(0)
         for bt in range(NBT):
-            c_job(0, bt)
+            nc.tensor.matmul(
+                out=lr_ps[:, 32 * bt : 32 * bt + 32],
+                lhsT=lhs_c[:, bt * P : (bt + 1) * P],
+                rhs=rhs_c[:, O : O + 32],
+                start=True,
+                stop=True,
+            )
+        nc.vector.tensor_copy(out=neg_lr[:], in_=lr_ps[:, 0:P].rearrange("p (t n) -> p t n", n=32)[:, :, 0])
+
+        for n in range(7):
+            d_job(n, "SV"[n % 2])
         for i in range(3):
             transposes(i, "SV")
             next_load(i)
             quantise(i, 0)
             quantise(i, 2)
-            spread(i + 1)
-
-        extra = {}
-        for i in range(2, n_units):
-            kind, view, t0, n = units[i]
-            ch = (t0 * P) // CHUNK
-            if ch + 1 >= O // CHUNK:
-                extra[i] = []
-            elif n == 2:
-                extra[i] = [(ch + 1, (0 if kind == "w" else 2) + (t0 % 4) // 2)]
-            else:
-                extra[i] = [(ch + 1, 0), (ch + 1, 1)] if kind == "w" else [(ch + 1, 2), (ch + 1, 3)]
+            for n in range(7 + 3 * i, 10 + 3 * i):
+                d_job(n, "S")
 
         for i in range(2, n_units):
             nxt = i + 1
@@ -234,19 +210,14 @@ def tile_optimizedlinear_kernel(
                 transposes(nxt, "S")
                 next_load(nxt)
                 quantise(nxt, 0)
-            jobs = extra[i]
             if nxt == n_units:
                 for bt in range(NBT):
                     mx_group(i, bt, 0, 256)
                     mx_group(i, bt, 256, 256)
                 break
             mx_group(i, 0)
-            if len(jobs) > 0:
-                c_job(jobs[0][0], jobs[0][1])
             mx_group(i, 1)
             if nxt < n_units:
                 quantise(nxt, 2)
             mx_group(i, 2)
-            if len(jobs) > 1:
-                c_job(jobs[1][0], jobs[1][1])
             mx_group(i, 3)

@@ -31,8 +31,9 @@ def tile_optimizedlinear_kernel(
         rawp = ctx.enter_context(tc.tile_pool(name="rawp", bufs=RAW_BUFS))
         grpp = ctx.enter_context(tc.tile_pool(name="grpp", bufs=2))
         codp = ctx.enter_context(tc.tile_pool(name="codp", bufs=3))
+        cpool = ctx.enter_context(tc.tile_pool(name="cpool", bufs=2))
         opool = ctx.enter_context(tc.tile_pool(name="opool", bufs=2))
-        psum = ctx.enter_context(tc.psum_pool(name="psum", bufs=8))
+        psum = ctx.enter_context(tc.psum_pool(name="psum", bufs=1))
         ctx.enter_context(tc.manual_schedule())
 
         x_v = input_data.rearrange("(t p) k -> p t k", p=P)
@@ -45,18 +46,24 @@ def tile_optimizedlinear_kernel(
             units += [("w", w_v, 4 * ch, 4), ("g", g_v, 4 * ch, 4)]
         n_units = len(units)
 
-        lhs_c = consts.tile([P, B], BF16)
-        nc.gpsimd.memset(lhs_c[:].bitcast(F32), 0.0)
-        nc.gpsimd.memset(lhs_c[32:33, :], -1.0)
-        rhs_c = consts.tile([P, O + 32], BF16)
-        nc.vector.memset(rhs_c[:].bitcast(F32), 0.0)
-        nc.vector.memset(rhs_c[0:1, O : O + 32], -1.0)
-        nc.sync.dma_start(out=lhs_c[0:1, :], in_=lr_samples.rearrange("(o n) -> o n", o=1))
-        nc.sync.dma_start(out=rhs_c[0:1, 0:O], in_=prev_bias_grad.rearrange("(o n) -> o n", o=1))
-        nc.sync.dma_start(out=rhs_c[32:33, 0:O], in_=bias.rearrange("(o n) -> o n", o=1))
         ident = consts.tile([P, P], F32)
         masks.make_identity(nc, ident[:])
+        ident_bf = consts.tile([P, P], BF16)
+        masks.make_identity(nc, ident_bf[:])
+        rows = consts.tile([P, CHUNK], BF16)
+        nc.vector.memset(rows[:], 0.0)
+        nc.sync.dma_start(out=rows[0:4, :], in_=bias.rearrange("(r n) -> r n", n=CHUNK))
+        nc.sync.dma_start(out=rows[4:8, :], in_=prev_bias_grad.rearrange("(r n) -> r n", n=CHUNK))
+        nc.sync.dma_start(out=rows[8:12, 0:P], in_=lr_samples.rearrange("(t p) -> t p", p=P))
         neg_lr = consts.tile([P, NBT], F32)
+        bias_bc = consts.tile([P, O], F32)
+        pbias_bc = consts.tile([P, O], F32)
+
+        made = []
+
+        def new_bank(name):
+            made.append(name)
+            return psum.tile([P, 512], F32, name=name, tag="ps%d" % ((len(made) - 1) % 8))
 
         raws = {}
 
@@ -80,7 +87,7 @@ def tile_optimizedlinear_kernel(
             b = 0
             for g in range(PASSES):
                 for h in range(n // 2):
-                    bank = psum.tile([P, 512], F32, name="bank%d_%d" % (i, b), tag="ps")
+                    bank = new_bank("bank%d_%d" % (i, b))
                     for j in range(2):
                         for u in range(2):
                             s = 2 * j + u
@@ -117,31 +124,27 @@ def tile_optimizedlinear_kernel(
                 in_=grouped[i][:, g0 : g0 + 2, :].rearrange("p g c -> p (g c)"),
             )
 
-        d_tiles = {}
+        c_tiles = {}
         o_tiles = {}
 
-        def d_job(n, eng):
-            ch, bt = n // NBT, n % NBT
-            if ch not in d_tiles:
-                d_tiles[ch] = consts.tile([P, NBT, CHUNK], F32, name="d%d" % ch)
-            d_ps = psum.tile([P, 512], F32, name="d_ps%d" % n, tag="ps")
-            nc.tensor.matmul(
-                out=d_ps[:],
-                lhsT=lhs_c[:, bt * P : (bt + 1) * P],
-                rhs=rhs_c[:, ch * CHUNK : (ch + 1) * CHUNK],
-                start=True,
-                stop=True,
+        def c_job(ch, bt):
+            if ch not in c_tiles:
+                c_tiles[ch] = cpool.tile([P, NBT, CHUNK], F32, name="c%d" % ch, tag="c")
+            cols = slice(ch * CHUNK, (ch + 1) * CHUNK)
+            nc.vector.scalar_tensor_tensor(
+                out=c_tiles[ch][:, bt, :],
+                in0=pbias_bc[:, cols],
+                scalar=neg_lr[:, bt : bt + 1],
+                in1=bias_bc[:, cols],
+                op0=ALU.mult,
+                op1=ALU.add,
             )
-            if eng == "S":
-                nc.scalar.copy(out=d_tiles[ch][:, bt, :], in_=d_ps[:])
-            else:
-                nc.vector.tensor_copy(out=d_tiles[ch][:, bt, :], in_=d_ps[:])
 
         def mx_group(i, bt, first=0, width=None):
             kind, view, t0, n = units[i]
             if width is None:
                 width = n * P
-            acc = psum.tile([P, 512], F32, name="acc%d_%d_%d" % (i, bt, first), tag="ps")
+            acc = new_bank("acc%d_%d_%d" % (i, bt, first))
             xi = bt // 2
             xs = slice((bt % 2) * P, (bt % 2) * P + P)
             for g in range(PASSES):
@@ -161,7 +164,7 @@ def tile_optimizedlinear_kernel(
             o_sl = o_tiles[ch][:, bt, lo : lo + width]
             if kind == "w":
                 nc.vector.tensor_tensor(
-                    out=o_sl, in0=acc[:, 0:width], in1=d_tiles[ch][:, bt, lo : lo + width], op=ALU.subtract
+                    out=o_sl, in0=acc[:, 0:width], in1=c_tiles[ch][:, bt, lo : lo + width], op=ALU.add
                 )
             else:
                 nc.vector.scalar_tensor_tensor(
@@ -183,26 +186,42 @@ def tile_optimizedlinear_kernel(
             if i + RAW_BUFS < n_units:
                 load(i + RAW_BUFS)
 
-        lr_ps = psum.tile([P, 512], F32, name="lr_ps", tag="ps")
-        for bt in range(NBT):
-            nc.tensor.matmul(
-                out=lr_ps[:, 32 * bt : 32 * bt + 32],
-                lhsT=lhs_c[:, bt * P : (bt + 1) * P],
-                rhs=rhs_c[:, O : O + 32],
-                start=True,
-                stop=True,
-            )
-        nc.vector.tensor_copy(out=neg_lr[:], in_=lr_ps[:, 0:P].rearrange("p (t n) -> p t n", n=32)[:, :, 0])
+        lr_ps = new_bank("lr_ps")
+        nc.tensor.matmul(out=lr_ps[:, 0:32], lhsT=rows[:, 0:P], rhs=ident_bf[:, 0:32], start=True, stop=True)
+        nc.vector.tensor_scalar_mul(out=neg_lr[:], in0=lr_ps[:, 8:12], scalar1=-1.0)
 
-        for n in range(7):
-            d_job(n, "SV"[n % 2])
+        def spread(ch):
+            for r, dst_t, eng in ((ch, bias_bc, "S"), (4 + ch, pbias_bc, "V" if ch == 0 else "S")):
+                bc = new_bank("bc%d" % r)
+                nc.tensor.matmul(
+                    out=bc[:], lhsT=ident_bf[:, r : r + 1].to_broadcast([P, P]), rhs=rows[:], start=True, stop=True
+                )
+                dst = dst_t[:, ch * CHUNK : (ch + 1) * CHUNK]
+                if eng == "S":
+                    nc.scalar.copy(out=dst, in_=bc[:])
+                else:
+                    nc.vector.tensor_copy(out=dst, in_=bc[:])
+
+        spread(0)
+        for bt in range(NBT):
+            c_job(0, bt)
         for i in range(3):
             transposes(i, "SV")
             next_load(i)
             quantise(i, 0)
             quantise(i, 2)
-            for n in range(7 + 3 * i, 10 + 3 * i):
-                d_job(n, "S")
+            spread(i + 1)
+
+        extra = {}
+        for i in range(2, n_units):
+            kind, view, t0, n = units[i]
+            ch = (t0 * P) // CHUNK
+            if ch + 1 >= O // CHUNK:
+                extra[i] = []
+            elif n == 2:
+                extra[i] = [(ch + 1, (0 if kind == "w" else 2) + (t0 % 4) // 2)]
+            else:
+                extra[i] = [(ch + 1, 0), (ch + 1, 1)] if kind == "w" else [(ch + 1, 2), (ch + 1, 3)]
 
         for i in range(2, n_units):
             nxt = i + 1
@@ -210,14 +229,19 @@ def tile_optimizedlinear_kernel(
                 transposes(nxt, "S")
                 next_load(nxt)
                 quantise(nxt, 0)
+            jobs = extra[i]
             if nxt == n_units:
                 for bt in range(NBT):
                     mx_group(i, bt, 0, 256)
                     mx_group(i, bt, 256, 256)
                 break
             mx_group(i, 0)
+            if len(jobs) > 0:
+                c_job(jobs[0][0], jobs[0][1])
             mx_group(i, 1)
             if nxt < n_units:
                 quantise(nxt, 2)
             mx_group(i, 2)
+            if len(jobs) > 1:
+                c_job(jobs[1][0], jobs[1][1])
             mx_group(i, 3)

@@ -33,8 +33,7 @@ def tile_optimizedlinear_kernel(
         codp = ctx.enter_context(tc.tile_pool(name="codp", bufs=3))
         cpool = ctx.enter_context(tc.tile_pool(name="cpool", bufs=2))
         opool = ctx.enter_context(tc.tile_pool(name="opool", bufs=2))
-        psum = ctx.enter_context(tc.psum_pool(name="psum", bufs=1))
-        ctx.enter_context(tc.manual_schedule())
+        psum = ctx.enter_context(tc.psum_pool(name="psum", bufs=8))
 
         x_v = input_data.rearrange("(t p) k -> p t k", p=P)
         w_v = weight.rearrange("(t p) k -> p t k", p=P)
@@ -59,12 +58,6 @@ def tile_optimizedlinear_kernel(
         bias_bc = consts.tile([P, O], F32)
         pbias_bc = consts.tile([P, O], F32)
 
-        made = []
-
-        def new_bank(name):
-            made.append(name)
-            return psum.tile([P, 512], F32, name=name, tag="ps%d" % ((len(made) - 1) % 8))
-
         raws = {}
 
         def load(i):
@@ -87,7 +80,7 @@ def tile_optimizedlinear_kernel(
             b = 0
             for g in range(PASSES):
                 for h in range(n // 2):
-                    bank = new_bank("bank%d_%d" % (i, b))
+                    bank = psum.tile([P, 512], F32, name="bank%d_%d" % (i, b), tag="ps")
                     for j in range(2):
                         for u in range(2):
                             s = 2 * j + u
@@ -144,7 +137,7 @@ def tile_optimizedlinear_kernel(
             kind, view, t0, n = units[i]
             if width is None:
                 width = n * P
-            acc = new_bank("acc%d_%d_%d" % (i, bt, first))
+            acc = psum.tile([P, 512], F32, name="acc%d_%d_%d" % (i, bt, first), tag="ps")
             xi = bt // 2
             xs = slice((bt % 2) * P, (bt % 2) * P + P)
             for g in range(PASSES):
@@ -186,13 +179,13 @@ def tile_optimizedlinear_kernel(
             if i + RAW_BUFS < n_units:
                 load(i + RAW_BUFS)
 
-        lr_ps = new_bank("lr_ps")
+        lr_ps = psum.tile([P, 512], F32, name="lr_ps", tag="ps")
         nc.tensor.matmul(out=lr_ps[:, 0:32], lhsT=rows[:, 0:P], rhs=ident_bf[:, 0:32], start=True, stop=True)
         nc.vector.tensor_scalar_mul(out=neg_lr[:], in0=lr_ps[:, 8:12], scalar1=-1.0)
 
         def spread(ch):
             for r, dst_t, eng in ((ch, bias_bc, "S"), (4 + ch, pbias_bc, "V" if ch == 0 else "S")):
-                bc = new_bank("bc%d" % r)
+                bc = psum.tile([P, 512], F32, name="bc%d" % r, tag="ps")
                 nc.tensor.matmul(
                     out=bc[:], lhsT=ident_bf[:, r : r + 1].to_broadcast([P, P]), rhs=rows[:], start=True, stop=True
                 )

from contextlib import ExitStack

import concourse.masks as masks
import concourse.mybir as mybir

F32 = mybir.dt.float32
BF16 = mybir.dt.bfloat16
U32 = mybir.dt.uint32
U8 = mybir.dt.uint8
FP8X4 = mybir.dt.float8_e4m3fn_x4
ALU = mybir.AluOpType

P = 128
B = 512
K = 2048
O = 2048
PASSES = K // 512
NBT = B // P
CHUNK = 512
FLOPS = 2 * 2 * B * K * O

RAW_BUFS = 5


def tile_optimizedlinear_kernel(
    tc, input_data, weight, bias, prev_grad, prev_bias_grad, lr_samples, out
):
    nc = tc.nc
    with ExitStack() as ctx:
        consts = ctx.enter_context(tc.tile_pool(name="consts", bufs=1))
        rawp = ctx.enter_context(tc.tile_pool(name="rawp", bufs=RAW_BUFS))
        grpp = ctx.enter_context(tc.tile_pool(name="grpp", bufs=2))
        codp = ctx.enter_context(tc.tile_pool(name="codp", bufs=3))
        cpool = ctx.enter_context(tc.tile_pool(name="cpool", bufs=2))
        opool = ctx.enter_context(tc.tile_pool(name="opool", bufs=2))
        psum = ctx.enter_context(tc.psum_pool(name="psum", bufs=8))

        x_v = input_data.rearrange("(t p) k -> p t k", p=P)
        w_v = weight.rearrange("(t p) k -> p t k", p=P)
        g_v = prev_grad.rearrange("(t p) k -> p t k", p=P)

        units = [("x", x_v, 0, 2), ("x", x_v, 2, 2)]
        units += [("w", w_v, 0, 2), ("w", w_v, 2, 2), ("g", g_v, 0, 2), ("g", g_v, 2, 2)]
        for ch in range(1, O // CHUNK):
            units += [("w", w_v, 4 * ch, 4), ("g", g_v, 4 * ch, 4)]
        n_units = len(units)

        ident = consts.tile([P, P], F32)
        masks.make_identity(nc, ident[:])
        ident_bf = consts.tile([P, P], BF16)
        masks.make_identity(nc, ident_bf[:])
        rows = consts.tile([P, CHUNK], BF16)
        nc.vector.memset(rows[:], 0.0)
        nc.sync.dma_start(out=rows[0:4, :], in_=bias.rearrange("(r n) -> r n", n=CHUNK))
        nc.sync.dma_start(out=rows[4:8, :], in_=prev_bias_grad.rearrange("(r n) -> r n", n=CHUNK))
        nc.sync.dma_start(out=rows[8:12, 0:P], in_=lr_samples.rearrange("(t p) -> t p", p=P))
        neg_lr = consts.tile([P, NBT], F32)
        bias_bc = consts.tile([P, O], F32)
        pbias_bc = consts.tile([P, O], F32)

        raws = {}

        def load(i):
            kind, view, t0, n = units[i]
            raw = rawp.tile([P, 4, K], BF16, name="raw%d" % i, tag="raw")
            nc.sync.dma_start(out=raw[:, 0:n, :], in_=view[:, t0 : t0 + n, :])
            raws[i] = raw

        grouped = {}
        codes = {}
        planes = {}

        def transposes(i, pattern):
            kind, view, t0, n = units[i]
            width = n * P
            raw_w = raws[i][:].bitcast(F32)
            grp = grpp.tile([P, PASSES, 4 * width], BF16, name="grp%d" % i, tag="grp", align_bytes=64)
            grouped[i] = grp
            grp_w = grp[:].bitcast(F32)
            b = 0
            for g in range(PASSES):
                for h in range(n // 2):
                    bank = psum.tile([P, 512], F32, name="bank%d_%d" % (i, b), tag="ps")
                    for j in range(2):
                        for u in range(2):
                            s = 2 * j + u
                            c0 = 256 * g + 128 * u
                            nc.tensor.transpose(
                                bank[:, s * P : (s + 1) * P], raw_w[:, 2 * h + j, c0 : c0 + P], ident[:]
                            )
                    dst = grp_w[:, g, 512 * h : 512 * h + 512].rearrange("p (j o u) -> p j o u", j=2, u=2)
                    src = bank[:].rearrange("p (j u o) -> p j o u", j=2, u=2)
                    if pattern[b % len(pattern)] == "S":
                        nc.scalar.copy(out=dst, in_=src)
                    else:
                        nc.vector.tensor_copy(out=dst, in_=src)
                    b += 1

        def alloc_codes(i):
            kind, view, t0, n = units[i]
            width = n * P
            if kind == "x":
                cod = consts.tile([P, PASSES, width], U32, name="xcod%d" % i, align_bytes=64)
                pla = consts.tile([P, PASSES, width], U8, name="xpla%d" % i, align_bytes=64)
            else:
                cod = codp.tile([P, PASSES, width], U32, name="cod%d" % i, tag="cod", align_bytes=64)
                pla = codp.tile([P, PASSES, width], U8, name="pla%d" % i, tag="pla", align_bytes=64)
            codes[i] = cod
            planes[i] = pla

        def quantise(i, g0):
            if g0 == 0:
                alloc_codes(i)
            nc.vector.quantize_mx(
                out=codes[i][:, g0 : g0 + 2, :].rearrange("p g n -> p (g n)").bitcast(FP8X4),
                scales=planes[i][:, g0 : g0 + 2, :].rearrange("p g n -> p (g n)"),
                in_=grouped[i][:, g0 : g0 + 2, :].rearrange("p g c -> p (g c)"),
            )

        c_tiles = {}
        o_tiles = {}

        def c_job(ch, bt):
            if ch not in c_tiles:
                c_tiles[ch] = cpool.tile([P, NBT, CHUNK], F32, name="c%d" % ch, tag="c")
            cols = slice(ch * CHUNK, (ch + 1) * CHUNK)
            nc.vector.scalar_tensor_tensor(
                out=c_tiles[ch][:, bt, :],
                in0=pbias_bc[:, cols],
                scalar=neg_lr[:, bt : bt + 1],
                in1=bias_bc[:, cols],
                op0=ALU.mult,
                op1=ALU.add,
            )

        def mx_group(i, bt, first=0, width=None):
            kind, view, t0, n = units[i]
            if width is None:
                width = n * P
            acc = psum.tile([P, 512], F32, name="acc%d_%d_%d" % (i, bt, first), tag="ps")
            xi = bt // 2
            xs = slice((bt % 2) * P, (bt % 2) * P + P)
            for g in range(PASSES):
                nc.tensor.matmul_mx(
                    out=acc[:, 0:width],
                    lhsT=codes[xi][:, g, xs].bitcast(FP8X4),
                    lhsT_scale=planes[xi][:, g, xs],
                    rhs=codes[i][:, g, first : first + width].bitcast(FP8X4),
                    rhs_scale=planes[i][:, g, first : first + width],
                    start=(g == 0),
                    stop=(g == PASSES - 1),
                )
            ch = (t0 * P) // CHUNK
            lo = t0 * P - ch * CHUNK + first
            if ch not in o_tiles:
                o_tiles[ch] = opool.tile([P, NBT, CHUNK], F32, name="o%d" % ch, tag="o")
            o_sl = o_tiles[ch][:, bt, lo : lo + width]
            if kind == "w":
                nc.vector.tensor_tensor(
                    out=o_sl, in0=acc[:, 0:width], in1=c_tiles[ch][:, bt, lo : lo + width], op=ALU.add
                )
            else:
                nc.vector.scalar_tensor_tensor(
                    out=o_sl,
                    in0=acc[:, 0:width],
                    scalar=neg_lr[:, bt : bt + 1],
                    in1=o_sl,
                    op0=ALU.mult,
                    op1=ALU.add,
                )
                nc.sync.dma_start(
                    out=out[bt * P : (bt + 1) * P, ch * CHUNK + lo : ch * CHUNK + lo + width], in_=o_sl
                )

        for i in range(RAW_BUFS):
            load(i)

        def next_load(i):
            if i + RAW_BUFS < n_units:
                load(i + RAW_BUFS)

        lr_ps = psum.tile([P, 512], F32, name="lr_ps", tag="ps")
        nc.tensor.matmul(out=lr_ps[:, 0:32], lhsT=rows[:, 0:P], rhs=ident_bf[:, 0:32], start=True, stop=True)
        nc.vector.tensor_scalar_mul(out=neg_lr[:], in0=lr_ps[:, 8:12], scalar1=-1.0)

        def spread(ch):
            for r, dst_t, eng in ((ch, bias_bc, "S"), (4 + ch, pbias_bc, "V" if ch == 0 else "S")):
                bc = psum.tile([P, 512], F32, name="bc%d" % r, tag="ps")
                nc.tensor.matmul(
                    out=bc[:], lhsT=ident_bf[:, r : r + 1].to_broadcast([P, P]), rhs=rows[:], start=True, stop=True
                )
                dst = dst_t[:, ch * CHUNK : (ch + 1) * CHUNK]
                if eng == "S":
                    nc.scalar.copy(out=dst, in_=bc[:])
                else:
                    nc.vector.tensor_copy(out=dst, in_=bc[:])

        spread(0)
        for bt in range(NBT):
            c_job(0, bt)
        for i in range(3):
            transposes(i, "SV")
            next_load(i)
            quantise(i, 0)
            quantise(i, 2)
            spread(i + 1)

        extra = {}
        for i in range(2, n_units):
            kind, view, t0, n = units[i]
            ch = (t0 * P) // CHUNK
            if ch + 1 >= O // CHUNK:
                extra[i] = []
            elif n == 2:
                extra[i] = [(ch + 1, (0 if kind == "w" else 2) + (t0 % 4) // 2)]
            else:
                extra[i] = [(ch + 1, 0), (ch + 1, 1)] if kind == "w" else [(ch + 1, 2), (ch + 1, 3)]

        for i in range(2, n_units):
            nxt = i + 1
            if nxt < n_units:
                transposes(nxt, "S")
                next_load(nxt)
                quantise(nxt, 0)
            jobs = extra[i]
            if nxt == n_units:
                for bt in range(NBT):
                    mx_group(i, bt, 0, 256)
                    mx_group(i, bt, 256, 256)
                break
            mx_group(i, 0)
            if len(jobs) > 0:
                c_job(jobs[0][0], jobs[0][1])
            mx_group(i, 1)
            if nxt < n_units:
                quantise(nxt, 2)
            mx_group(i, 2)
            if len(jobs) > 1:
                c_job(jobs[1][0], jobs[1][1])
            mx_group(i, 3)
